import numpy as np
import ml_dtypes

BF16 = ml_dtypes.bfloat16


def bf(x):
    return np.asarray(x, np.float32).astype(BF16)


def f32(x):
    return np.asarray(x, np.float32)


def f64(x):
    return np.asarray(x).astype(np.float64)


def striped(idx):
    return np.tile(idx.reshape(-1, 16).T, (8, 1))


D, V, N, SQ, NB, NH, DH = 768, 2048, 1024, 256, 4, 6, 128
EPS = 1e-5


def setup_inputs():
    r = np.random.standard_normal
    return {
        "tok": f32(r((D, V))),
        "pos": f32(0.5 * r((D, SQ))),
        "wq": bf(r((D, D)) / np.sqrt(D)),
        "bq": f32(0.1 * r((D, 1))),
        "wk": bf(r((D, D)) / np.sqrt(D)),
        "wv": bf(2.0 * r((D, D)) / np.sqrt(D)),
        "bv": f32(0.1 * r((D, 1))),
        "wo": bf(2.0 * r((D, D)) / np.sqrt(D)),
        "bo": f32(0.1 * r((D, 1))),
        "gain": f32(1.0 + 0.1 * r((D, 1))),
        "shift": f32(0.1 * r((D, 1))),
        "offs": striped(np.random.permutation(np.tile(np.arange(V), 2))[:N]),
    }


def reference(tok, pos, wq, bq, wk, wv, bv, wo, bo, gain, shift, offs):
    idx = offs[:16].T.reshape(-1)
    x = f64(tok)[:, idx] + np.tile(f64(pos), (1, NB))
    q = (f64(wq).T @ x + f64(bq)).reshape(NH, DH, NB, SQ)
    k = (f64(wk).T @ x).reshape(NH, DH, NB, SQ)
    v = (f64(wv).T @ x + f64(bv)).reshape(NH, DH, NB, SQ)
    sc = np.einsum('hdrt,hdru->hrtu', q, k) / np.sqrt(DH)
    e = np.exp(sc - sc.max(axis=-1, keepdims=True))
    att = e / e.sum(axis=-1, keepdims=True)
    ctx = np.einsum('hrtu,hdru->hdrt', att, v).reshape(D, N)
    z = f64(wo).T @ ctx + f64(bo) + x
    mu = z.mean(axis=0, keepdims=True)
    var = np.square(z - mu).mean(axis=0, keepdims=True)
    return (z - mu) / np.sqrt(var + EPS) * f64(gain) + f64(shift)

@@ -1,0 +1,210 @@
+import math
+
+import concourse.mybir as mybir
+from concourse.masks import make_identity
+
+F32 = mybir.dt.float32
+BF16 = mybir.dt.bfloat16
+U16 = mybir.dt.uint16
+ALU = mybir.AluOpType
+ACT = mybir.ActivationFunctionType
+AX = mybir.AxisListType
+
+P = 128
+D = 768
+V = 2048
+N = 1024
+SQ = 256
+NB = N // SQ
+NH = D // P
+CB = D // P
+HALF = 512
+VW = D // 2
+EPS = 1e-5
+SCALE = 1.0 / math.sqrt(P)
+
+FLOPS = 4 * 2 * D * D * N + 2 * 2 * NH * NB * SQ * SQ * P
+
+
+def tile_bert_b_kernel(tc, tok, pos, wq, bq, wk, wv, bv, wo, bo, gain, shift, offs, out):
+    nc = tc.nc
+    with (
+        tc.tile_pool(name="held", bufs=1) as held,
+        tc.psum_pool(name="psum_proj", bufs=2) as psum_proj,
+        tc.psum_pool(name="psum_sc", bufs=2) as psum_sc,
+        tc.psum_pool(name="psum_att", bufs=1) as psum_att,
+        tc.psum_pool(name="psum_stat", bufs=2) as psum_stat,
+    ):
+        offsets = held.tile([P, N // 16], U16, name="offsets")
+        nc.sync.dma_start(offsets[:], offs)
+
+        rows = held.tile([P, P], F32, name="rows")
+        nc.gpsimd.memset(rows[:], 0.0)
+        for i, vec in enumerate((bq, bo, gain, shift)):
+            nc.sync.dma_start(rows[i * CB:(i + 1) * CB, :], vec.rearrange("(b p) o -> b (p o)", p=P))
+        bv_bc = held.tile([P, D], F32, name="bv_bc")
+        nc.scalar.dma_start(bv_bc[:], bv.rearrange("d o -> (d o)").partition_broadcast(P))
+
+        x32 = [held.tile([P, N], F32, name=f"x32_{c}") for c in range(CB)]
+        xb = [held.tile([P, N], BF16, name=f"xb_{c}") for c in range(CB)]
+
+        with tc.tile_pool(name="table", bufs=1) as table:
+            pos_t = table.tile([P, CB, SQ], F32, name="pos_t")
+            nc.scalar.dma_start(pos_t[:], pos.rearrange("(c p) t -> p c t", p=P))
+            tok_t = [table.tile([P, V], F32, name=f"tok_{c}") for c in range(CB)]
+            for c in range(CB):
+                queue = nc.sync if c % 2 == 0 else nc.scalar
+                queue.dma_start(tok_t[c][:], tok[c * P:(c + 1) * P, :])
+
+            w_t = {}
+            for i, (name, w) in enumerate((("wv", wv), ("wq", wq), ("wk", wk), ("wo", wo))):
+                w_t[name] = held.tile([P, CB, D], BF16, name=name + "_t")
+                queue = nc.sync if i % 2 == 0 else nc.scalar
+                queue.dma_start(w_t[name][:], w.rearrange("(c p) m -> p c m", p=P))
+
+            ident_f = held.tile([P, P], F32, name="ident_f")
+            make_identity(nc, ident_f[:])
+            ident_b = held.tile([P, P], BF16, name="ident_b")
+            make_identity(nc, ident_b[:])
+            ones_f = held.tile([P, P], F32, name="ones_f")
+            nc.gpsimd.memset(ones_f[:], 1.0)
+            eps_col = held.tile([P, 1], F32, name="eps_col")
+            nc.gpsimd.memset(eps_col[:], EPS)
+
+            cols_ps = psum_stat.tile([P, P], F32, tag="stat")
+            nc.tensor.transpose(cols_ps[:], rows[:], ident_f[:])
+            cols = held.tile([P, P], F32, name="cols")
+            nc.vector.tensor_copy(cols[:], cols_ps[:])
+            bq_col = [cols[:, 0 * CB + b:0 * CB + b + 1] for b in range(CB)]
+            bo_col = [cols[:, 1 * CB + b:1 * CB + b + 1] for b in range(CB)]
+            gain_col = [cols[:, 2 * CB + b:2 * CB + b + 1] for b in range(CB)]
+            shift_col = [cols[:, 3 * CB + b:3 * CB + b + 1] for b in range(CB)]
+
+            for c in range(CB):
+                for r in range(NB):
+                    nc.vector.tensor_tensor(
+                        x32[c][:, r * SQ:(r + 1) * SQ],
+                        tok_t[c][:].indirect(offsets[:, r * (SQ // 16):(r + 1) * (SQ // 16)]),
+                        pos_t[:, c, :],
+                        ALU.add,
+                    )
+                nc.scalar.copy(xb[c][:], x32[c][:])
+
+        with (
+            tc.tile_pool(name="acts", bufs=1) as acts,
+            tc.tile_pool(name="work", bufs=3) as work,
+            tc.tile_pool(name="small", bufs=4) as small,
+        ):
+            vT = [acts.tile([P, D], BF16, name=f"vT_{jb}") for jb in range(N // P)]
+            for jb in range(N // P):
+                for hf in range(2):
+                    v_ps = psum_proj.tile([P, HALF], F32, tag="proj")
+                    for c in range(CB):
+                        nc.tensor.matmul(
+                            v_ps[:, :VW],
+                            lhsT=xb[c][:, jb * P:(jb + 1) * P],
+                            rhs=w_t["wv"][:, c, hf * VW:(hf + 1) * VW],
+                            start=(c == 0),
+                            stop=(c == CB - 1),
+                        )
+                    nc.vector.tensor_tensor(
+                        vT[jb][:, hf * VW:(hf + 1) * VW], v_ps[:, :VW], bv_bc[:, hf * VW:(hf + 1) * VW], ALU.add
+                    )
+
+            ctx = [acts.tile([P, N], BF16, name=f"ctx_{h}") for h in range(NH)]
+            for h in range(NH):
+                q_h = work.tile([P, N], BF16, tag="q_h", bufs=2)
+                k_h = work.tile([P, N], BF16, tag="k_h", bufs=2)
+                for half in range(N // HALF):
+                    span = slice(half * HALF, (half + 1) * HALF)
+                    q_ps = psum_proj.tile([P, HALF], F32, tag="proj")
+                    for c in range(CB):
+                        nc.tensor.matmul(
+                            q_ps[:], lhsT=w_t["wq"][:, c, h * P:(h + 1) * P], rhs=xb[c][:, span],
+                            start=(c == 0), stop=(c == CB - 1),
+                        )
+                    nc.scalar.activation(q_h[:, span], q_ps[:], ACT.Identity, bias=bq_col[h])
+                    k_ps = psum_proj.tile([P, HALF], F32, tag="proj")
+                    for c in range(CB):
+                        nc.tensor.matmul(
+                            k_ps[:], lhsT=w_t["wk"][:, c, h * P:(h + 1) * P], rhs=xb[c][:, span],
+                            start=(c == 0), stop=(c == CB - 1),
+                        )
+                    nc.scalar.copy(k_h[:, span], k_ps[:])
+
+                for r in range(NB):
+                    seq = slice(r * SQ, (r + 1) * SQ)
+                    sc = psum_sc.tile([P, 2, SQ], F32, tag="sc")
+                    for tb in range(2):
+                        nc.tensor.matmul(
+                            sc[:, tb, :],
+                            lhsT=q_h[:, r * SQ + tb * P:r * SQ + (tb + 1) * P],
+                            rhs=k_h[:, seq],
+                            start=True, stop=True,
+                        )
+                    top = small.tile([P, 2], F32, tag="top")
+                    nc.vector.tensor_reduce(top[:], sc[:], axis=AX.X, op=ALU.max)
+                    shift_exp = small.tile([P, 2], F32, tag="shift_exp")
+                    nc.vector.tensor_scalar_mul(shift_exp[:], top[:], -SCALE)
+                    e = work.tile([P, 2, SQ], F32, tag="e")
+                    e_sum = small.tile([P, 2], F32, tag="e_sum")
+                    for tb in range(2):
+                        nc.scalar.activation(
+                            e[:, tb, :], sc[:, tb, :], ACT.Exp,
+                            bias=shift_exp[:, tb:tb + 1], scale=SCALE, accum_out=e_sum[:, tb:tb + 1],
+                        )
+                    e_inv = small.tile([P, 2], F32, tag="e_inv")
+                    nc.vector.reciprocal(e_inv[:], e_sum[:])
+                    att = work.tile([P, 2, SQ], BF16, tag="att")
+                    for tb in range(2):
+                        nc.vector.tensor_scalar_mul(att[:, tb, :], e[:, tb, :], e_inv[:, tb:tb + 1])
+                    attT_ps = psum_att.tile([P, 2, SQ], BF16, tag="attT_ps")
+                    for ub in range(2):
+                        for tb in range(2):
+                            nc.tensor.transpose(
+                                attT_ps[:, ub, tb * P:(tb + 1) * P], att[:, tb, ub * P:(ub + 1) * P], ident_b[:]
+                            )
+                    attT = work.tile([P, 2, SQ], BF16, tag="attT")
+                    nc.vector.tensor_copy(attT[:], attT_ps[:])
+                    ctx_ps = psum_att.tile([P, SQ], F32, tag="ctx_ps")
+                    for ub in range(2):
+                        nc.tensor.matmul(
+                            ctx_ps[:],
+                            lhsT=vT[r * 2 + ub][:, h * P:(h + 1) * P],
+                            rhs=attT[:, ub, :],
+                            start=(ub == 0), stop=(ub == 1),
+                        )
+                    nc.scalar.copy(ctx[h][:, seq], ctx_ps[:])
+
+            for half in range(N // HALF):
+                span = slice(half * HALF, (half + 1) * HALF)
+                z = [work.tile([P, HALF], F32, name=f"z_{m}", bufs=2) for m in range(CB)]
+                z_sum = psum_stat.tile([P, HALF], F32, tag="stat")
+                for m in range(CB):
+                    o_ps = psum_proj.tile([P, HALF], F32, tag="proj")
+                    for c in range(CB):
+                        nc.tensor.matmul(
+                            o_ps[:], lhsT=w_t["wo"][:, c, m * P:(m + 1) * P], rhs=ctx[c][:, span],
+                            start=(c == 0), stop=(c == CB - 1),
+                        )
+                    nc.vector.scalar_tensor_tensor(
+                        z[m][:], o_ps[:], bo_col[m], x32[m][:, span], op0=ALU.add, op1=ALU.add
+                    )
+                for m in range(CB):
+                    nc.tensor.matmul(z_sum[:], lhsT=ones_f[:], rhs=z[m][:], start=(m == 0), stop=(m == CB - 1))
+                sq_sum = psum_stat.tile([P, HALF], F32, tag="stat")
+                for m in range(CB):
+                    nc.vector.scalar_tensor_tensor(
+                        z[m][:], z_sum[:], -1.0 / D, z[m][:], op0=ALU.mult, op1=ALU.add
+                    )
+                    sq = work.tile([P, HALF], F32, tag="sq")
+                    nc.scalar.activation(sq[:], z[m][:], ACT.Square)
+                    nc.tensor.matmul(sq_sum[:], lhsT=ones_f[:], rhs=sq[:], start=(m == 0), stop=(m == CB - 1))
+                rstd = work.tile([P, HALF], F32, tag="rstd", bufs=2)
+                nc.scalar.activation(rstd[:], sq_sum[:], ACT.Abs_reciprocal_sqrt, bias=eps_col[:], scale=1.0 / D)
+                for m in range(CB):
+                    normed = work.tile([P, HALF], F32, tag="normed")
+                    nc.vector.tensor_mul(normed[:], z[m][:], rstd[:])
+                    res = work.tile([P, HALF], F32, tag="res")
+                    nc.scalar.activation(res[:], normed[:], ACT.Identity, bias=shift_col[m], scale=gain_col[m])
+                    nc.sync.dma_start(out[m * P:(m + 1) * P, span], res[:])

@@ -179,7 +179,7 @@ def tile_bert_b_kernel(tc, tok, pos, wq, bq, wk, wv, bv, wo, bo, gain, shift, of
             for half in range(N // HALF):
                 span = slice(half * HALF, (half + 1) * HALF)
                 z = [work.tile([P, HALF], F32, name=f"z_{m}", bufs=2) for m in range(CB)]
-                z_sum = psum_stat.tile([P, HALF], F32, tag="stat")
+                z_acc = work.tile([P, HALF], F32, tag="z_acc", bufs=2)
                 for m in range(CB):
                     o_ps = psum_proj.tile([P, HALF], F32, tag="proj")
                     for c in range(CB):
@@ -190,16 +190,24 @@ def tile_bert_b_kernel(tc, tok, pos, wq, bq, wk, wv, bv, wo, bo, gain, shift, of
                     nc.vector.scalar_tensor_tensor(
                         z[m][:], o_ps[:], bo_col[m], x32[m][:, span], op0=ALU.add, op1=ALU.add
                     )
-                for m in range(CB):
-                    nc.tensor.matmul(z_sum[:], lhsT=ones_f[:], rhs=z[m][:], start=(m == 0), stop=(m == CB - 1))
-                sq_sum = psum_stat.tile([P, HALF], F32, tag="stat")
+                    if m > 0:
+                        nc.gpsimd.tensor_add(z_acc[:], z[0][:] if m == 1 else z_acc[:], z[m][:])
+                z_sum = psum_stat.tile([P, HALF], F32, tag="stat")
+                nc.tensor.matmul(z_sum[:], lhsT=ones_f[:], rhs=z_acc[:], start=True, stop=True)
+                sq_acc = work.tile([P, HALF], F32, tag="sq_acc", bufs=2)
+                sq_first = None
                 for m in range(CB):
                     nc.vector.scalar_tensor_tensor(
                         z[m][:], z_sum[:], -1.0 / D, z[m][:], op0=ALU.mult, op1=ALU.add
                     )
                     sq = work.tile([P, HALF], F32, tag="sq")
                     nc.scalar.activation(sq[:], z[m][:], ACT.Square)
-                    nc.tensor.matmul(sq_sum[:], lhsT=ones_f[:], rhs=sq[:], start=(m == 0), stop=(m == CB - 1))
+                    if m == 0:
+                        sq_first = sq
+                    else:
+                        nc.gpsimd.tensor_add(sq_acc[:], sq_first[:] if m == 1 else sq_acc[:], sq[:])
+                sq_sum = psum_stat.tile([P, HALF], F32, tag="stat")
+                nc.tensor.matmul(sq_sum[:], lhsT=ones_f[:], rhs=sq_acc[:], start=True, stop=True)
                 rstd = work.tile([P, HALF], F32, tag="rstd", bufs=2)
                 nc.scalar.activation(rstd[:], sq_sum[:], ACT.Abs_reciprocal_sqrt, bias=eps_col[:], scale=1.0 / D)
                 for m in range(CB):

@@ -20,6 +20,8 @@ NH = D // P
 CB = D // P
 HALF = 512
 VW = D // 2
+LW = SQ // 16
+TB = N // P
 EPS = 1e-5
 SCALE = 1.0 / math.sqrt(P)
 
@@ -30,189 +32,206 @@ def tile_bert_b_kernel(tc, tok, pos, wq, bq, wk, wv, bv, wo, bo, gain, shift, of
     nc = tc.nc
     with (
         tc.tile_pool(name="held", bufs=1) as held,
+        tc.tile_pool(name="work", bufs=3) as work,
+        tc.tile_pool(name="small", bufs=4) as small,
         tc.psum_pool(name="psum_proj", bufs=2) as psum_proj,
-        tc.psum_pool(name="psum_sc", bufs=2) as psum_sc,
-        tc.psum_pool(name="psum_att", bufs=1) as psum_att,
-        tc.psum_pool(name="psum_stat", bufs=2) as psum_stat,
     ):
         offsets = held.tile([P, N // 16], U16, name="offsets")
         nc.sync.dma_start(offsets[:], offs)
 
         rows = held.tile([P, P], F32, name="rows")
         nc.gpsimd.memset(rows[:], 0.0)
-        for i, vec in enumerate((bq, bo, gain, shift)):
-            nc.sync.dma_start(rows[i * CB:(i + 1) * CB, :], vec.rearrange("(b p) o -> b (p o)", p=P))
+        for i, vec in enumerate((bq, gain, shift)):
+            nc.gpsimd.dma_start(rows[i * CB:(i + 1) * CB, :], vec.rearrange("(b p) o -> b (p o)", p=P))
         bv_bc = held.tile([P, D], F32, name="bv_bc")
-        nc.scalar.dma_start(bv_bc[:], bv.rearrange("d o -> (d o)").partition_broadcast(P))
+        nc.gpsimd.dma_start(bv_bc[:], bv.rearrange("d o -> (d o)").partition_broadcast(P))
+        bo_bc = held.tile([P, D], F32, name="bo_bc")
+        nc.gpsimd.dma_start(bo_bc[:], bo.rearrange("d o -> (d o)").partition_broadcast(P))
 
+        ident_f = held.tile([P, P], F32, name="ident_f")
+        make_identity(nc, ident_f[:])
+        ident_b = held.tile([P, P], BF16, name="ident_b")
+        make_identity(nc, ident_b[:])
+        eps_col = held.tile([P, 1], F32, name="eps_col")
+        nc.gpsimd.memset(eps_col[:], EPS)
+
+        w_t = {
+            name: [held.tile([P, D], BF16, name=f"{name}_{c}") for c in range(CB)]
+            for name in ("wq", "wk", "wv", "wo")
+        }
         x32 = [held.tile([P, N], F32, name=f"x32_{c}") for c in range(CB)]
         xb = [held.tile([P, N], BF16, name=f"xb_{c}") for c in range(CB)]
+        xT = held.tile([P, TB, D], F32, name="xT")
+        q_t = [held.tile([P, N], BF16, name=f"q_{h}") for h in range(NH)]
+        k_t = [held.tile([P, N], BF16, name=f"k_{h}") for h in range(NH)]
+        vT = [held.tile([P, D], BF16, name=f"vT_{jb}") for jb in range(TB)]
+        ctx = [held.tile([P, N], BF16, name=f"ctx_{h}") for h in range(NH)]
 
-        with tc.tile_pool(name="table", bufs=1) as table:
-            pos_t = table.tile([P, CB, SQ], F32, name="pos_t")
-            nc.scalar.dma_start(pos_t[:], pos.rearrange("(c p) t -> p c t", p=P))
+        with (
+            tc.tile_pool(name="table", bufs=1) as table,
+            tc.psum_pool(name="psum_first", bufs=1) as psum_first,
+        ):
             tok_t = [table.tile([P, V], F32, name=f"tok_{c}") for c in range(CB)]
+            pos_t = [table.tile([P, SQ], F32, name=f"pos_{c}") for c in range(CB)]
             for c in range(CB):
-                queue = nc.sync if c % 2 == 0 else nc.scalar
-                queue.dma_start(tok_t[c][:], tok[c * P:(c + 1) * P, :])
+                block = slice(c * P, (c + 1) * P)
+                nc.sync.dma_start(pos_t[c][:], pos[block, :])
+                nc.sync.dma_start(tok_t[c][:], tok[block, :])
+                nc.sync.dma_start(w_t["wq"][c][:], wq[block, :])
+            for name, w in (("wv", wv), ("wk", wk), ("wo", wo)):
+                for c in range(CB):
+                    nc.sync.dma_start(w_t[name][c][:], w[c * P:(c + 1) * P, :])
 
-            w_t = {}
-            for i, (name, w) in enumerate((("wv", wv), ("wq", wq), ("wk", wk), ("wo", wo))):
-                w_t[name] = held.tile([P, CB, D], BF16, name=name + "_t")
-                queue = nc.sync if i % 2 == 0 else nc.scalar
-                queue.dma_start(w_t[name][:], w.rearrange("(c p) m -> p c m", p=P))
-
-            ident_f = held.tile([P, P], F32, name="ident_f")
-            make_identity(nc, ident_f[:])
-            ident_b = held.tile([P, P], BF16, name="ident_b")
-            make_identity(nc, ident_b[:])
-            ones_f = held.tile([P, P], F32, name="ones_f")
-            nc.gpsimd.memset(ones_f[:], 1.0)
-            eps_col = held.tile([P, 1], F32, name="eps_col")
-            nc.gpsimd.memset(eps_col[:], EPS)
-
-            cols_ps = psum_stat.tile([P, P], F32, tag="stat")
-            nc.tensor.transpose(cols_ps[:], rows[:], ident_f[:])
-            cols = held.tile([P, P], F32, name="cols")
-            nc.vector.tensor_copy(cols[:], cols_ps[:])
-            bq_col = [cols[:, 0 * CB + b:0 * CB + b + 1] for b in range(CB)]
-            bo_col = [cols[:, 1 * CB + b:1 * CB + b + 1] for b in range(CB)]
-            gain_col = [cols[:, 2 * CB + b:2 * CB + b + 1] for b in range(CB)]
-            shift_col = [cols[:, 3 * CB + b:3 * CB + b + 1] for b in range(CB)]
-
+            q_first = [psum_first.tile([P, HALF], F32, name=f"q_first_{h}") for h in range(NH)]
             for c in range(CB):
                 for r in range(NB):
                     nc.vector.tensor_tensor(
                         x32[c][:, r * SQ:(r + 1) * SQ],
-                        tok_t[c][:].indirect(offsets[:, r * (SQ // 16):(r + 1) * (SQ // 16)]),
-                        pos_t[:, c, :],
+                        tok_t[c][:].indirect(offsets[:, r * LW:(r + 1) * LW]),
+                        pos_t[c][:],
                         ALU.add,
                     )
-                nc.scalar.copy(xb[c][:], x32[c][:])
+                    if r % 2 == 1:
+                        span = slice((r - 1) * SQ, (r + 1) * SQ)
+                        nc.scalar.copy(xb[c][:, span], x32[c][:, span])
+                for h in range(NH):
+                    nc.tensor.matmul(
+                        q_first[h][:], lhsT=w_t["wq"][c][:, h * P:(h + 1) * P], rhs=xb[c][:, :HALF],
+                        start=(c == 0), stop=(c == CB - 1),
+                    )
+                for g in range(TB // 4):
+                    xT_ps = psum_proj.tile([P, 4, P], F32, tag="proj")
+                    for i in range(4):
+                        jb = 4 * g + i
+                        nc.tensor.transpose(xT_ps[:, i, :], x32[c][:, jb * P:(jb + 1) * P], ident_f[:])
+                    nc.scalar.copy(xT[:, 4 * g:4 * g + 4, c * P:(c + 1) * P], xT_ps[:])
+
+            cols_ps = psum_proj.tile([P, P], F32, tag="proj")
+            nc.tensor.transpose(cols_ps[:], rows[:], ident_f[:])
+            cols = held.tile([P, P], F32, name="cols")
+            nc.vector.tensor_copy(cols[:], cols_ps[:])
+            bq_col = [cols[:, 0 * CB + b:0 * CB + b + 1] for b in range(CB)]
+            gain_col = [cols[:, 1 * CB + b:1 * CB + b + 1] for b in range(CB)]
+            shift_col = [cols[:, 2 * CB + b:2 * CB + b + 1] for b in range(CB)]
+
+            for h in range(NH):
+                nc.scalar.activation(q_t[h][:, :HALF], q_first[h][:], ACT.Identity, bias=bq_col[h])
+
+        for jb in range(TB):
+            nc.gpsimd.tensor_add(xT[:, jb, :], xT[:, jb, :], bo_bc[:])
 
         with (
-            tc.tile_pool(name="acts", bufs=1) as acts,
-            tc.tile_pool(name="work", bufs=3) as work,
-            tc.tile_pool(name="small", bufs=4) as small,
+            tc.tile_pool(name="last", bufs=3) as last,
+            tc.psum_pool(name="psum_sc", bufs=2) as psum_sc,
+            tc.psum_pool(name="psum_att", bufs=1) as psum_att,
+            tc.psum_pool(name="psum_back", bufs=2) as psum_back,
         ):
-            vT = [acts.tile([P, D], BF16, name=f"vT_{jb}") for jb in range(N // P)]
-            for jb in range(N // P):
+            def project(name, h, span):
+                acc = psum_proj.tile([P, HALF], F32, name="acc", tag="proj")
+                for c in range(CB):
+                    nc.tensor.matmul(
+                        acc[:], lhsT=w_t[name][c][:, h * P:(h + 1) * P], rhs=xb[c][:, span],
+                        start=(c == 0), stop=(c == CB - 1),
+                    )
+                return acc
+
+            def attend(h, r):
+                seq = slice(r * SQ, (r + 1) * SQ)
+                sc = psum_sc.tile([P, 2, SQ], F32, tag="sc")
+                for tb in range(2):
+                    nc.tensor.matmul(
+                        sc[:, tb, :],
+                        lhsT=q_t[h][:, r * SQ + tb * P:r * SQ + (tb + 1) * P],
+                        rhs=k_t[h][:, seq],
+                        start=True, stop=True,
+                    )
+                top = small.tile([P, 2], F32, tag="top")
+                nc.vector.tensor_reduce(top[:], sc[:], axis=AX.X, op=ALU.max)
+                shift_exp = small.tile([P, 2], F32, tag="shift_exp")
+                nc.vector.tensor_scalar_mul(shift_exp[:], top[:], -SCALE)
+                e = work.tile([P, 2, SQ], F32, tag="e")
+                e_sum = small.tile([P, 2], F32, tag="e_sum")
+                for tb in range(2):
+                    nc.scalar.activation(
+                        e[:, tb, :], sc[:, tb, :], ACT.Exp,
+                        bias=shift_exp[:, tb:tb + 1], scale=SCALE, accum_out=e_sum[:, tb:tb + 1],
+                    )
+                e_inv = small.tile([P, 2], F32, tag="e_inv")
+                nc.vector.reciprocal(e_inv[:], e_sum[:])
+                att = work.tile([P, 2, SQ], BF16, tag="att")
+                for tb in range(2):
+                    nc.vector.tensor_scalar_mul(att[:, tb, :], e[:, tb, :], e_inv[:, tb:tb + 1])
+                attT_ps = psum_att.tile([P, 2, SQ], BF16, tag="attT_ps")
+                for ub in range(2):
+                    for tb in range(2):
+                        nc.tensor.transpose(
+                            attT_ps[:, ub, tb * P:(tb + 1) * P], att[:, tb, ub * P:(ub + 1) * P], ident_b[:]
+                        )
+                attT = work.tile([P, 2, SQ], BF16, tag="attT")
+                nc.vector.tensor_copy(attT[:], attT_ps[:])
+                ctx_ps = psum_att.tile([P, SQ], F32, tag="ctx_ps")
+                for ub in range(2):
+                    nc.tensor.matmul(
+                        ctx_ps[:],
+                        lhsT=vT[r * 2 + ub][:, h * P:(h + 1) * P],
+                        rhs=attT[:, ub, :],
+                        start=(ub == 0), stop=(ub == 1),
+                    )
+                nc.scalar.copy(ctx[h][:, seq], ctx_ps[:])
+
+            def finish(jb):
+                z = last.tile([P, D], F32, tag="z")
+                stats = small.tile([P, 2, 6], F32, tag="stats")
                 for hf in range(2):
-                    v_ps = psum_proj.tile([P, HALF], F32, tag="proj")
+                    feats = slice(hf * VW, (hf + 1) * VW)
+                    o_ps = psum_proj.tile([P, VW], F32, tag="proj")
                     for c in range(CB):
                         nc.tensor.matmul(
-                            v_ps[:, :VW],
-                            lhsT=xb[c][:, jb * P:(jb + 1) * P],
-                            rhs=w_t["wv"][:, c, hf * VW:(hf + 1) * VW],
-                            start=(c == 0),
-                            stop=(c == CB - 1),
+                            o_ps[:], lhsT=ctx[c][:, jb * P:(jb + 1) * P], rhs=w_t["wo"][c][:, feats],
+                            start=(c == 0), stop=(c == CB - 1),
                         )
-                    nc.vector.tensor_tensor(
-                        vT[jb][:, hf * VW:(hf + 1) * VW], v_ps[:, :VW], bv_bc[:, hf * VW:(hf + 1) * VW], ALU.add
-                    )
+                    nc.vector.tensor_tensor(z[:, feats], o_ps[:], xT[:, jb, feats], ALU.add)
+                    nc.vector.bn_stats(stats[:, hf, :], z[:, feats])
+                mean_var = small.tile([P, 2], F32, tag="mean_var")
+                nc.vector.bn_aggr(mean_var[:], stats[:].rearrange("p a b -> p (a b)"))
+                rstd = small.tile([P, 1], F32, tag="rstd")
+                nc.scalar.activation(rstd[:], mean_var[:, 1:2], ACT.Abs_reciprocal_sqrt, bias=eps_col[:])
+                normed = last.tile([P, D], F32, tag="normed")
+                nc.vector.tensor_scalar(
+                    normed[:], z[:], mean_var[:, 0:1], rstd[:], op0=ALU.subtract, op1=ALU.mult
+                )
+                res = last.tile([P, CB, P], F32, tag="res")
+                for g in range(2):
+                    back = psum_back.tile([P, 3, P], F32, tag="back")
+                    for i in range(3):
+                        m = 3 * g + i
+                        nc.tensor.transpose(back[:, i, :], normed[:, m * P:(m + 1) * P], ident_f[:])
+                    for i in range(3):
+                        m = 3 * g + i
+                        nc.scalar.activation(
+                            res[:, m, :], back[:, i, :], ACT.Identity, bias=shift_col[m], scale=gain_col[m]
+                        )
+                nc.sync.dma_start(out.rearrange("(m p) j -> p m j", p=P)[:, :, jb * P:(jb + 1) * P], res[:])
 
-            ctx = [acts.tile([P, N], BF16, name=f"ctx_{h}") for h in range(NH)]
+            for jb in range(TB):
+                for hf in range(2):
+                    feats = slice(hf * VW, (hf + 1) * VW)
+                    v_ps = psum_proj.tile([P, VW], F32, tag="proj")
+                    for c in range(CB):
+                        nc.tensor.matmul(
+                            v_ps[:], lhsT=xb[c][:, jb * P:(jb + 1) * P], rhs=w_t["wv"][c][:, feats],
+                            start=(c == 0), stop=(c == CB - 1),
+                        )
+                    nc.vector.tensor_tensor(vT[jb][:, feats], v_ps[:], bv_bc[:, feats], ALU.add)
+
             for h in range(NH):
-                q_h = work.tile([P, N], BF16, tag="q_h", bufs=2)
-                k_h = work.tile([P, N], BF16, tag="k_h", bufs=2)
                 for half in range(N // HALF):
                     span = slice(half * HALF, (half + 1) * HALF)
-                    q_ps = psum_proj.tile([P, HALF], F32, tag="proj")
-                    for c in range(CB):
-                        nc.tensor.matmul(
-                            q_ps[:], lhsT=w_t["wq"][:, c, h * P:(h + 1) * P], rhs=xb[c][:, span],
-                            start=(c == 0), stop=(c == CB - 1),
-                        )
-                    nc.scalar.activation(q_h[:, span], q_ps[:], ACT.Identity, bias=bq_col[h])
-                    k_ps = psum_proj.tile([P, HALF], F32, tag="proj")
-                    for c in range(CB):
-                        nc.tensor.matmul(
-                            k_ps[:], lhsT=w_t["wk"][:, c, h * P:(h + 1) * P], rhs=xb[c][:, span],
-                            start=(c == 0), stop=(c == CB - 1),
-                        )
-                    nc.scalar.copy(k_h[:, span], k_ps[:])
-
+                    if half > 0:
+                        nc.scalar.activation(q_t[h][:, span], project("wq", h, span)[:], ACT.Identity, bias=bq_col[h])
+                    nc.scalar.copy(k_t[h][:, span], project("wk", h, span)[:])
                 for r in range(NB):
-                    seq = slice(r * SQ, (r + 1) * SQ)
-                    sc = psum_sc.tile([P, 2, SQ], F32, tag="sc")
-                    for tb in range(2):
-                        nc.tensor.matmul(
-                            sc[:, tb, :],
-                            lhsT=q_h[:, r * SQ + tb * P:r * SQ + (tb + 1) * P],
-                            rhs=k_h[:, seq],
-                            start=True, stop=True,
-                        )
-                    top = small.tile([P, 2], F32, tag="top")
-                    nc.vector.tensor_reduce(top[:], sc[:], axis=AX.X, op=ALU.max)
-                    shift_exp = small.tile([P, 2], F32, tag="shift_exp")
-                    nc.vector.tensor_scalar_mul(shift_exp[:], top[:], -SCALE)
-                    e = work.tile([P, 2, SQ], F32, tag="e")
-                    e_sum = small.tile([P, 2], F32, tag="e_sum")
-                    for tb in range(2):
-                        nc.scalar.activation(
-                            e[:, tb, :], sc[:, tb, :], ACT.Exp,
-                            bias=shift_exp[:, tb:tb + 1], scale=SCALE, accum_out=e_sum[:, tb:tb + 1],
-                        )
-                    e_inv = small.tile([P, 2], F32, tag="e_inv")
-                    nc.vector.reciprocal(e_inv[:], e_sum[:])
-                    att = work.tile([P, 2, SQ], BF16, tag="att")
-                    for tb in range(2):
-                        nc.vector.tensor_scalar_mul(att[:, tb, :], e[:, tb, :], e_inv[:, tb:tb + 1])
-                    attT_ps = psum_att.tile([P, 2, SQ], BF16, tag="attT_ps")
-                    for ub in range(2):
-                        for tb in range(2):
-                            nc.tensor.transpose(
-                                attT_ps[:, ub, tb * P:(tb + 1) * P], att[:, tb, ub * P:(ub + 1) * P], ident_b[:]
-                            )
-                    attT = work.tile([P, 2, SQ], BF16, tag="attT")
-                    nc.vector.tensor_copy(attT[:], attT_ps[:])
-                    ctx_ps = psum_att.tile([P, SQ], F32, tag="ctx_ps")
-                    for ub in range(2):
-                        nc.tensor.matmul(
-                            ctx_ps[:],
-                            lhsT=vT[r * 2 + ub][:, h * P:(h + 1) * P],
-                            rhs=attT[:, ub, :],
-                            start=(ub == 0), stop=(ub == 1),
-                        )
-                    nc.scalar.copy(ctx[h][:, seq], ctx_ps[:])
+                    attend(h, r)
 
-            for half in range(N // HALF):
-                span = slice(half * HALF, (half + 1) * HALF)
-                z = [work.tile([P, HALF], F32, name=f"z_{m}", bufs=2) for m in range(CB)]
-                z_acc = work.tile([P, HALF], F32, tag="z_acc", bufs=2)
-                for m in range(CB):
-                    o_ps = psum_proj.tile([P, HALF], F32, tag="proj")
-                    for c in range(CB):
-                        nc.tensor.matmul(
-                            o_ps[:], lhsT=w_t["wo"][:, c, m * P:(m + 1) * P], rhs=ctx[c][:, span],
-                            start=(c == 0), stop=(c == CB - 1),
-                        )
-                    nc.vector.scalar_tensor_tensor(
-                        z[m][:], o_ps[:], bo_col[m], x32[m][:, span], op0=ALU.add, op1=ALU.add
-                    )
-                    if m > 0:
-                        nc.gpsimd.tensor_add(z_acc[:], z[0][:] if m == 1 else z_acc[:], z[m][:])
-                z_sum = psum_stat.tile([P, HALF], F32, tag="stat")
-                nc.tensor.matmul(z_sum[:], lhsT=ones_f[:], rhs=z_acc[:], start=True, stop=True)
-                sq_acc = work.tile([P, HALF], F32, tag="sq_acc", bufs=2)
-                sq_first = None
-                for m in range(CB):
-                    nc.vector.scalar_tensor_tensor(
-                        z[m][:], z_sum[:], -1.0 / D, z[m][:], op0=ALU.mult, op1=ALU.add
-                    )
-                    sq = work.tile([P, HALF], F32, tag="sq")
-                    nc.scalar.activation(sq[:], z[m][:], ACT.Square)
-                    if m == 0:
-                        sq_first = sq
-                    else:
-                        nc.gpsimd.tensor_add(sq_acc[:], sq_first[:] if m == 1 else sq_acc[:], sq[:])
-                sq_sum = psum_stat.tile([P, HALF], F32, tag="stat")
-                nc.tensor.matmul(sq_sum[:], lhsT=ones_f[:], rhs=sq_acc[:], start=True, stop=True)
-                rstd = work.tile([P, HALF], F32, tag="rstd", bufs=2)
-                nc.scalar.activation(rstd[:], sq_sum[:], ACT.Abs_reciprocal_sqrt, bias=eps_col[:], scale=1.0 / D)
-                for m in range(CB):
-                    normed = work.tile([P, HALF], F32, tag="normed")
-                    nc.vector.tensor_mul(normed[:], z[m][:], rstd[:])
-                    res = work.tile([P, HALF], F32, tag="res")
-                    nc.scalar.activation(res[:], normed[:], ACT.Identity, bias=shift_col[m], scale=gain_col[m])
-                    nc.sync.dma_start(out[m * P:(m + 1) * P, span], res[:])
+            for jb in range(TB):
+                finish(jb)

@@ -19,9 +19,13 @@ NB = N // SQ
 NH = D // P
 CB = D // P
 HALF = 512
-VW = D // 2
 LW = SQ // 16
 TB = N // P
+VW = D // 2
+UNITS = NB * NH
+PAIRS = UNITS // 2
+V_UNITS = TB * 2
+FIRST_OUT = 2 * (PAIRS - 3) + 1
 EPS = 1e-5
 SCALE = 1.0 / math.sqrt(P)
 
@@ -34,7 +38,6 @@ def tile_bert_b_kernel(tc, tok, pos, wq, bq, wk, wv, bv, wo, bo, gain, shift, of
         tc.tile_pool(name="held", bufs=1) as held,
         tc.tile_pool(name="work", bufs=3) as work,
         tc.tile_pool(name="small", bufs=4) as small,
-        tc.psum_pool(name="psum_proj", bufs=2) as psum_proj,
     ):
         offsets = held.tile([P, N // 16], U16, name="offsets")
         nc.sync.dma_start(offsets[:], offs)
@@ -52,14 +55,13 @@ def tile_bert_b_kernel(tc, tok, pos, wq, bq, wk, wv, bv, wo, bo, gain, shift, of
         make_identity(nc, ident_f[:])
         ident_b = held.tile([P, P], BF16, name="ident_b")
         make_identity(nc, ident_b[:])
-        eps_col = held.tile([P, 1], F32, name="eps_col")
-        nc.gpsimd.memset(eps_col[:], EPS)
+        minus_half = held.tile([P, 1], F32, name="minus_half")
+        nc.gpsimd.memset(minus_half[:], -0.5)
 
         w_t = {
             name: [held.tile([P, D], BF16, name=f"{name}_{c}") for c in range(CB)]
             for name in ("wq", "wk", "wv", "wo")
         }
-        x32 = [held.tile([P, N], F32, name=f"x32_{c}") for c in range(CB)]
         xb = [held.tile([P, N], BF16, name=f"xb_{c}") for c in range(CB)]
         xT = held.tile([P, TB, D], F32, name="xT")
         q_t = [held.tile([P, N], BF16, name=f"q_{h}") for h in range(NH)]
@@ -70,15 +72,17 @@ def tile_bert_b_kernel(tc, tok, pos, wq, bq, wk, wv, bv, wo, bo, gain, shift, of
         with (
             tc.tile_pool(name="table", bufs=1) as table,
             tc.psum_pool(name="psum_first", bufs=1) as psum_first,
+            tc.psum_pool(name="psum_x", bufs=2) as psum_x,
         ):
             tok_t = [table.tile([P, V], F32, name=f"tok_{c}") for c in range(CB)]
             pos_t = [table.tile([P, SQ], F32, name=f"pos_{c}") for c in range(CB)]
+            x32 = [table.tile([P, N], F32, name=f"x32_{c}") for c in range(CB)]
             for c in range(CB):
                 block = slice(c * P, (c + 1) * P)
                 nc.sync.dma_start(pos_t[c][:], pos[block, :])
                 nc.sync.dma_start(tok_t[c][:], tok[block, :])
                 nc.sync.dma_start(w_t["wq"][c][:], wq[block, :])
-            for name, w in (("wv", wv), ("wk", wk), ("wo", wo)):
+            for name, w in (("wk", wk), ("wv", wv), ("wo", wo)):
                 for c in range(CB):
                     nc.sync.dma_start(w_t[name][c][:], w[c * P:(c + 1) * P, :])
 
@@ -100,13 +104,13 @@ def tile_bert_b_kernel(tc, tok, pos, wq, bq, wk, wv, bv, wo, bo, gain, shift, of
                         start=(c == 0), stop=(c == CB - 1),
                     )
                 for g in range(TB // 4):
-                    xT_ps = psum_proj.tile([P, 4, P], F32, tag="proj")
+                    xT_ps = psum_x.tile([P, 4, P], F32, tag="xT_ps")
                     for i in range(4):
                         jb = 4 * g + i
                         nc.tensor.transpose(xT_ps[:, i, :], x32[c][:, jb * P:(jb + 1) * P], ident_f[:])
                     nc.scalar.copy(xT[:, 4 * g:4 * g + 4, c * P:(c + 1) * P], xT_ps[:])
 
-            cols_ps = psum_proj.tile([P, P], F32, tag="proj")
+            cols_ps = psum_x.tile([P, P], F32, tag="xT_ps")
             nc.tensor.transpose(cols_ps[:], rows[:], ident_f[:])
             cols = held.tile([P, P], F32, name="cols")
             nc.vector.tensor_copy(cols[:], cols_ps[:])
@@ -122,29 +126,55 @@ def tile_bert_b_kernel(tc, tok, pos, wq, bq, wk, wv, bv, wo, bo, gain, shift, of
 
         with (
             tc.tile_pool(name="last", bufs=3) as last,
+            tc.psum_pool(name="psum_large", bufs=4) as psum_large,
             tc.psum_pool(name="psum_sc", bufs=2) as psum_sc,
-            tc.psum_pool(name="psum_att", bufs=1) as psum_att,
-            tc.psum_pool(name="psum_back", bufs=2) as psum_back,
+            tc.psum_pool(name="psum_flip", bufs=1) as psum_flip,
+            tc.psum_pool(name="psum_ctx", bufs=1) as psum_ctx,
         ):
-            def project(name, h, span):
-                acc = psum_proj.tile([P, HALF], F32, name="acc", tag="proj")
+            def where(u):
+                pair, second = divmod(u, 2)
+                half, h = divmod(pair, NH)
+                return h, 2 * half + second
+
+            def project(name, pair):
+                half, h = divmod(pair, NH)
+                acc = psum_large.tile([P, HALF], F32, name="acc", tag="large")
                 for c in range(CB):
                     nc.tensor.matmul(
-                        acc[:], lhsT=w_t[name][c][:, h * P:(h + 1) * P], rhs=xb[c][:, span],
+                        acc[:], lhsT=w_t[name][c][:, h * P:(h + 1) * P], rhs=xb[c][:, half * HALF:(half + 1) * HALF],
                         start=(c == 0), stop=(c == CB - 1),
                     )
                 return acc
 
-            def attend(h, r):
-                seq = slice(r * SQ, (r + 1) * SQ)
+            def project_q(pair):
+                half, h = divmod(pair, NH)
+                nc.scalar.activation(
+                    q_t[h][:, half * HALF:(half + 1) * HALF], project("wq", pair)[:], ACT.Identity, bias=bq_col[h]
+                )
+
+            def project_k(pair):
+                half, h = divmod(pair, NH)
+                nc.scalar.copy(k_t[h][:, half * HALF:(half + 1) * HALF], project("wk", pair)[:])
+
+            sc_of = {}
+            e_of = {}
+            att_of = {}
+            attT_of = {}
+
+            def scores(u):
+                h, r = where(u)
                 sc = psum_sc.tile([P, 2, SQ], F32, tag="sc")
                 for tb in range(2):
                     nc.tensor.matmul(
                         sc[:, tb, :],
                         lhsT=q_t[h][:, r * SQ + tb * P:r * SQ + (tb + 1) * P],
-                        rhs=k_t[h][:, seq],
+                        rhs=k_t[h][:, r * SQ:(r + 1) * SQ],
                         start=True, stop=True,
                     )
+                sc_of[u] = sc
+
+            def softmax_top(u):
+                sc = sc_of[u]
                 top = small.tile([P, 2], F32, tag="top")
                 nc.vector.tensor_reduce(top[:], sc[:], axis=AX.X, op=ALU.max)
                 shift_exp = small.tile([P, 2], F32, tag="shift_exp")
@@ -156,20 +186,33 @@ def tile_bert_b_kernel(tc, tok, pos, wq, bq, wk, wv, bv, wo, bo, gain, shift, of
                         e[:, tb, :], sc[:, tb, :], ACT.Exp,
                         bias=shift_exp[:, tb:tb + 1], scale=SCALE, accum_out=e_sum[:, tb:tb + 1],
                     )
+                e_of[u] = (e, e_sum)
+
+            def softmax_bottom(u):
+                e, e_sum = e_of[u]
                 e_inv = small.tile([P, 2], F32, tag="e_inv")
                 nc.vector.reciprocal(e_inv[:], e_sum[:])
                 att = work.tile([P, 2, SQ], BF16, tag="att")
                 for tb in range(2):
                     nc.vector.tensor_scalar_mul(att[:, tb, :], e[:, tb, :], e_inv[:, tb:tb + 1])
-                attT_ps = psum_att.tile([P, 2, SQ], BF16, tag="attT_ps")
+                att_of[u] = att
+
+            def flip(u):
+                att = att_of[u]
+                attT_ps = psum_flip.tile([P, 2, SQ], BF16, tag="attT_ps")
                 for ub in range(2):
                     for tb in range(2):
                         nc.tensor.transpose(
                             attT_ps[:, ub, tb * P:(tb + 1) * P], att[:, tb, ub * P:(ub + 1) * P], ident_b[:]
                         )
                 attT = work.tile([P, 2, SQ], BF16, tag="attT")
-                nc.vector.tensor_copy(attT[:], attT_ps[:])
-                ctx_ps = psum_att.tile([P, SQ], F32, tag="ctx_ps")
+                nc.scalar.copy(attT[:], attT_ps[:])
+                attT_of[u] = attT
+
+            def context(u):
+                h, r = where(u)
+                attT = attT_of[u]
+                ctx_ps = psum_ctx.tile([P, SQ], F32, tag="ctx_ps")
                 for ub in range(2):
                     nc.tensor.matmul(
                         ctx_ps[:],
@@ -177,32 +220,67 @@ def tile_bert_b_kernel(tc, tok, pos, wq, bq, wk, wv, bv, wo, bo, gain, shift, of
                         rhs=attT[:, ub, :],
                         start=(ub == 0), stop=(ub == 1),
                     )
-                nc.scalar.copy(ctx[h][:, seq], ctx_ps[:])
+                nc.scalar.copy(ctx[h][:, r * SQ:(r + 1) * SQ], ctx_ps[:])
 
-            def finish(jb):
-                z = last.tile([P, D], F32, tag="z")
+            def value_unit(n):
+                group, k = divmod(n, TB // 2)
+                half, hf = divmod(group, 2)
+                jb = half * (TB // 2) + k
+                feats = slice(hf * VW, (hf + 1) * VW)
+                v_ps = psum_large.tile([P, VW], F32, tag="large")
+                for c in range(CB):
+                    nc.tensor.matmul(
+                        v_ps[:], lhsT=xb[c][:, jb * P:(jb + 1) * P], rhs=w_t["wv"][c][:, feats],
+                        start=(c == 0), stop=(c == CB - 1),
+                    )
+                nc.vector.tensor_tensor(vT[jb][:, feats], v_ps[:], bv_bc[:, feats], ALU.add)
+
+            z_of = {}
+            moments_of = {}
+            normed_of = {}
+
+            def out_unit(jb, hf):
+                if hf == 0:
+                    z_of[jb] = last.tile([P, D], F32, name="z", tag="z")
+                z = z_of[jb]
+                feats = slice(hf * VW, (hf + 1) * VW)
+                o_ps = psum_large.tile([P, VW], F32, tag="large")
+                for c in range(CB):
+                    nc.tensor.matmul(
+                        o_ps[:], lhsT=ctx[c][:, jb * P:(jb + 1) * P], rhs=w_t["wo"][c][:, feats],
+                        start=(c == 0), stop=(c == CB - 1),
+                    )
+                nc.vector.tensor_tensor(z[:, feats], o_ps[:], xT[:, jb, feats], ALU.add)
+
+            def moments(jb):
+                z = z_of[jb]
                 stats = small.tile([P, 2, 6], F32, tag="stats")
                 for hf in range(2):
-                    feats = slice(hf * VW, (hf + 1) * VW)
-                    o_ps = psum_proj.tile([P, VW], F32, tag="proj")
-                    for c in range(CB):
-                        nc.tensor.matmul(
-                            o_ps[:], lhsT=ctx[c][:, jb * P:(jb + 1) * P], rhs=w_t["wo"][c][:, feats],
-                            start=(c == 0), stop=(c == CB - 1),
-                        )
-                    nc.vector.tensor_tensor(z[:, feats], o_ps[:], xT[:, jb, feats], ALU.add)
-                    nc.vector.bn_stats(stats[:, hf, :], z[:, feats])
+                    nc.vector.bn_stats(stats[:, hf, :], z[:, hf * VW:(hf + 1) * VW])
                 mean_var = small.tile([P, 2], F32, tag="mean_var")
                 nc.vector.bn_aggr(mean_var[:], stats[:].rearrange("p a b -> p (a b)"))
+                var_eps = small.tile([P, 1], F32, tag="var_eps")
+                nc.gpsimd.tensor_scalar_add(var_eps[:], mean_var[:, 1:2], EPS)
                 rstd = small.tile([P, 1], F32, tag="rstd")
-                nc.scalar.activation(rstd[:], mean_var[:, 1:2], ACT.Abs_reciprocal_sqrt, bias=eps_col[:])
-                normed = last.tile([P, D], F32, tag="normed")
-                nc.vector.tensor_scalar(
-                    normed[:], z[:], mean_var[:, 0:1], rstd[:], op0=ALU.subtract, op1=ALU.mult
+                nc.gpsimd.tensor_tensor(rstd[:], var_eps[:], minus_half[:], ALU.pow)
+                minus_mu_rstd = small.tile([P, 1], F32, tag="minus_mu_rstd")
+                nc.gpsimd.tensor_scalar(
+                    minus_mu_rstd[:], mean_var[:, 0:1], rstd[:], -1.0, op0=ALU.mult, op1=ALU.mult
                 )
+                moments_of[jb] = (rstd, minus_mu_rstd)
+
+            def normalise(jb):
+                z = z_of[jb]
+                rstd, minus_mu_rstd = moments_of[jb]
+                normed = last.tile([P, D], F32, tag="normed")
+                nc.scalar.activation(normed[:], z[:], ACT.Identity, bias=minus_mu_rstd[:], scale=rstd[:])
+                normed_of[jb] = normed
+
+            def store_block(jb):
+                normed = normed_of[jb]
                 res = last.tile([P, CB, P], F32, tag="res")
                 for g in range(2):
-                    back = psum_back.tile([P, 3, P], F32, tag="back")
+                    back = psum_large.tile([P, 3, P], F32, tag="large")
                     for i in range(3):
                         m = 3 * g + i
                         nc.tensor.transpose(back[:, i, :], normed[:, m * P:(m + 1) * P], ident_f[:])
@@ -213,25 +291,34 @@ def tile_bert_b_kernel(tc, tok, pos, wq, bq, wk, wv, bv, wo, bo, gain, shift, of
                         )
                 nc.sync.dma_start(out.rearrange("(m p) j -> p m j", p=P)[:, :, jb * P:(jb + 1) * P], res[:])
 
-            for jb in range(TB):
-                for hf in range(2):
-                    feats = slice(hf * VW, (hf + 1) * VW)
-                    v_ps = psum_proj.tile([P, VW], F32, tag="proj")
-                    for c in range(CB):
-                        nc.tensor.matmul(
-                            v_ps[:], lhsT=xb[c][:, jb * P:(jb + 1) * P], rhs=w_t["wv"][c][:, feats],
-                            start=(c == 0), stop=(c == CB - 1),
-                        )
-                    nc.vector.tensor_tensor(vT[jb][:, feats], v_ps[:], bv_bc[:, feats], ALU.add)
-
-            for h in range(NH):
-                for half in range(N // HALF):
-                    span = slice(half * HALF, (half + 1) * HALF)
-                    if half > 0:
-                        nc.scalar.activation(q_t[h][:, span], project("wq", h, span)[:], ACT.Identity, bias=bq_col[h])
-                    nc.scalar.copy(k_t[h][:, span], project("wk", h, span)[:])
-                for r in range(NB):
-                    attend(h, r)
-
-            for jb in range(TB):
-                finish(jb)
+            for s in range(-5, FIRST_OUT + TB + 3):
+                pair, odd = divmod(s, 2)
+                jb = s - FIRST_OUT
+                if 0 <= s < UNITS:
+                    flip(s)
+                if 0 <= s + 2 < UNITS:
+                    softmax_top(s + 2)
+                if 0 <= jb - 2 < TB:
+                    normalise(jb - 2)
+                if 0 <= jb - 1 < TB:
+                    moments(jb - 1)
+                if odd and 0 <= pair + 3 < PAIRS:
+                    project_k(pair + 3)
+                if not odd and NH <= pair + 2 < PAIRS:
+                    project_q(pair + 2)
+                if not odd and 0 <= s + 4 < V_UNITS:
+                    value_unit(s + 4)
+                if 0 <= jb < TB:
+                    out_unit(jb, 0)
+                if 0 <= s + 2 < UNITS:
+                    softmax_bottom(s + 2)
+                if not odd and 0 <= s + 4 < V_UNITS:
+                    value_unit(s + 5)
+                if 0 <= jb < TB:
+                    out_unit(jb, 1)
+                if 0 <= s < UNITS:
+                    context(s)
+                if 0 <= s + 3 < UNITS:
+                    scores(s + 3)
+                if 0 <= jb - 3 < TB:
+                    store_block(jb - 3)

@@ -25,6 +25,7 @@ VW = D // 2
 UNITS = NB * NH
 PAIRS = UNITS // 2
 V_UNITS = TB * 2
+EARLY = 8
 FIRST_OUT = 2 * (PAIRS - 3) + 1
 EPS = 1e-5
 SCALE = 1.0 / math.sqrt(P)
@@ -45,7 +46,7 @@ def tile_bert_b_kernel(tc, tok, pos, wq, bq, wk, wv, bv, wo, bo, gain, shift, of
         rows = held.tile([P, P], F32, name="rows")
         nc.gpsimd.memset(rows[:], 0.0)
         for i, vec in enumerate((bq, gain, shift)):
-            nc.gpsimd.dma_start(rows[i * CB:(i + 1) * CB, :], vec.rearrange("(b p) o -> b (p o)", p=P))
+            nc.scalar.dma_start(rows[i * CB:(i + 1) * CB, :], vec.rearrange("(b p) o -> b (p o)", p=P))
         bv_bc = held.tile([P, D], F32, name="bv_bc")
         nc.gpsimd.dma_start(bv_bc[:], bv.rearrange("d o -> (d o)").partition_broadcast(P))
         bo_bc = held.tile([P, D], F32, name="bo_bc")
@@ -58,10 +59,20 @@ def tile_bert_b_kernel(tc, tok, pos, wq, bq, wk, wv, bv, wo, bo, gain, shift, of
         minus_half = held.tile([P, 1], F32, name="minus_half")
         nc.gpsimd.memset(minus_half[:], -0.5)
 
+        cols = held.tile([P, P], F32, name="cols")
+        with tc.psum_pool(name="psum_cols", bufs=1) as psum_cols:
+            cols_ps = psum_cols.tile([P, P], F32, name="cols_ps")
+            nc.tensor.transpose(cols_ps[:], rows[:], ident_f[:])
+            nc.scalar.copy(cols[:], cols_ps[:])
+        bq_col = [cols[:, 0 * CB + b:0 * CB + b + 1] for b in range(CB)]
+        gain_col = [cols[:, 1 * CB + b:1 * CB + b + 1] for b in range(CB)]
+        shift_col = [cols[:, 2 * CB + b:2 * CB + b + 1] for b in range(CB)]
+
         w_t = {
             name: [held.tile([P, D], BF16, name=f"{name}_{c}") for c in range(CB)]
             for name in ("wq", "wk", "wv", "wo")
         }
+        x32 = [held.tile([P, N], F32, name=f"x32_{c}") for c in range(CB)]
         xb = [held.tile([P, N], BF16, name=f"xb_{c}") for c in range(CB)]
         xT = held.tile([P, TB, D], F32, name="xT")
         q_t = [held.tile([P, N], BF16, name=f"q_{h}") for h in range(NH)]
@@ -72,21 +83,21 @@ def tile_bert_b_kernel(tc, tok, pos, wq, bq, wk, wv, bv, wo, bo, gain, shift, of
         with (
             tc.tile_pool(name="table", bufs=1) as table,
             tc.psum_pool(name="psum_first", bufs=1) as psum_first,
-            tc.psum_pool(name="psum_x", bufs=2) as psum_x,
         ):
             tok_t = [table.tile([P, V], F32, name=f"tok_{c}") for c in range(CB)]
             pos_t = [table.tile([P, SQ], F32, name=f"pos_{c}") for c in range(CB)]
-            x32 = [table.tile([P, N], F32, name=f"x32_{c}") for c in range(CB)]
             for c in range(CB):
                 block = slice(c * P, (c + 1) * P)
                 nc.sync.dma_start(pos_t[c][:], pos[block, :])
                 nc.sync.dma_start(tok_t[c][:], tok[block, :])
-                nc.sync.dma_start(w_t["wq"][c][:], wq[block, :])
+                if c > 0:
+                    nc.sync.dma_start(w_t["wq"][c - 1][:], wq[(c - 1) * P:c * P, :])
+            nc.sync.dma_start(w_t["wq"][CB - 1][:], wq[(CB - 1) * P:, :])
             for name, w in (("wk", wk), ("wv", wv), ("wo", wo)):
                 for c in range(CB):
                     nc.sync.dma_start(w_t[name][c][:], w[c * P:(c + 1) * P, :])
 
-            q_first = [psum_first.tile([P, HALF], F32, name=f"q_first_{h}") for h in range(NH)]
+            q_first = [psum_first.tile([P, HALF], F32, name=f"q_first_{pair}") for pair in range(EARLY)]
             for c in range(CB):
                 for r in range(NB):
                     nc.vector.tensor_tensor(
@@ -98,31 +109,21 @@ def tile_bert_b_kernel(tc, tok, pos, wq, bq, wk, wv, bv, wo, bo, gain, shift, of
                     if r % 2 == 1:
                         span = slice((r - 1) * SQ, (r + 1) * SQ)
                         nc.scalar.copy(xb[c][:, span], x32[c][:, span])
-                for h in range(NH):
+                for pair in range(EARLY):
+                    half, h = divmod(pair, NH)
                     nc.tensor.matmul(
-                        q_first[h][:], lhsT=w_t["wq"][c][:, h * P:(h + 1) * P], rhs=xb[c][:, :HALF],
+                        q_first[pair][:],
+                        lhsT=w_t["wq"][c][:, h * P:(h + 1) * P], rhs=xb[c][:, half * HALF:(half + 1) * HALF],
                         start=(c == 0), stop=(c == CB - 1),
                     )
-                for g in range(TB // 4):
-                    xT_ps = psum_x.tile([P, 4, P], F32, tag="xT_ps")
-                    for i in range(4):
-                        jb = 4 * g + i
-                        nc.tensor.transpose(xT_ps[:, i, :], x32[c][:, jb * P:(jb + 1) * P], ident_f[:])
-                    nc.scalar.copy(xT[:, 4 * g:4 * g + 4, c * P:(c + 1) * P], xT_ps[:])
 
-            cols_ps = psum_x.tile([P, P], F32, tag="xT_ps")
-            nc.tensor.transpose(cols_ps[:], rows[:], ident_f[:])
-            cols = held.tile([P, P], F32, name="cols")
-            nc.vector.tensor_copy(cols[:], cols_ps[:])
-            bq_col = [cols[:, 0 * CB + b:0 * CB + b + 1] for b in range(CB)]
-            gain_col = [cols[:, 1 * CB + b:1 * CB + b + 1] for b in range(CB)]
-            shift_col = [cols[:, 2 * CB + b:2 * CB + b + 1] for b in range(CB)]
-
-            for h in range(NH):
-                nc.scalar.activation(q_t[h][:, :HALF], q_first[h][:], ACT.Identity, bias=bq_col[h])
-
-        for jb in range(TB):
-            nc.gpsimd.tensor_add(xT[:, jb, :], xT[:, jb, :], bo_bc[:])
+            for pair in range(EARLY):
+                half, h = divmod(pair, NH)
+                q_out = q_t[h][:, half * HALF:(half + 1) * HALF]
+                if pair % 2 == 0:
+                    nc.scalar.activation(q_out, q_first[pair][:], ACT.Identity, bias=bq_col[h])
+                else:
+                    nc.vector.tensor_scalar_add(q_out, q_first[pair][:], bq_col[h])
 
         with (
             tc.tile_pool(name="last", bufs=3) as last,
@@ -131,6 +132,15 @@ def tile_bert_b_kernel(tc, tok, pos, wq, bq, wk, wv, bv, wo, bo, gain, shift, of
             tc.psum_pool(name="psum_flip", bufs=1) as psum_flip,
             tc.psum_pool(name="psum_ctx", bufs=1) as psum_ctx,
         ):
+            def flip_x(c):
+                bo_block = bo_bc[:, c * P:(c + 1) * P].unsqueeze(1).to_broadcast([P, 4, P])
+                for g in range(TB // 4):
+                    xT_ps = psum_large.tile([P, 4, P], F32, tag="large")
+                    for i in range(4):
+                        jb = 4 * g + i
+                        nc.tensor.transpose(xT_ps[:, i, :], x32[c][:, jb * P:(jb + 1) * P], ident_f[:])
+                    nc.vector.tensor_tensor(xT[:, 4 * g:4 * g + 4, c * P:(c + 1) * P], xT_ps[:], bo_block, ALU.add)
+
             def where(u):
                 pair, second = divmod(u, 2)
                 half, h = divmod(pair, NH)
@@ -291,9 +301,11 @@ def tile_bert_b_kernel(tc, tok, pos, wq, bq, wk, wv, bv, wo, bo, gain, shift, of
                         )
                 nc.sync.dma_start(out.rearrange("(m p) j -> p m j", p=P)[:, :, jb * P:(jb + 1) * P], res[:])
 
-            for s in range(-5, FIRST_OUT + TB + 3):
+            for s in range(-CB, FIRST_OUT + TB + 3):
                 pair, odd = divmod(s, 2)
                 jb = s - FIRST_OUT
+                if s < 0:
+                    flip_x(s + CB)
                 if 0 <= s < UNITS:
                     flip(s)
                 if 0 <= s + 2 < UNITS:
@@ -304,7 +316,7 @@ def tile_bert_b_kernel(tc, tok, pos, wq, bq, wk, wv, bv, wo, bo, gain, shift, of
                     moments(jb - 1)
                 if odd and 0 <= pair + 3 < PAIRS:
                     project_k(pair + 3)
-                if not odd and NH <= pair + 2 < PAIRS:
+                if not odd and EARLY <= pair + 2 < PAIRS:
                     project_q(pair + 2)
                 if not odd and 0 <= s + 4 < V_UNITS:
                     value_unit(s + 4)

@@ -127,6 +127,7 @@ def tile_bert_b_kernel(tc, tok, pos, wq, bq, wk, wv, bv, wo, bo, gain, shift, of
 
         with (
             tc.tile_pool(name="last", bufs=3) as last,
+            tc.tile_pool(name="leaving", bufs=4) as leaving,
             tc.psum_pool(name="psum_large", bufs=4) as psum_large,
             tc.psum_pool(name="psum_sc", bufs=2) as psum_sc,
             tc.psum_pool(name="psum_flip", bufs=1) as psum_flip,
@@ -251,8 +252,11 @@ def tile_bert_b_kernel(tc, tok, pos, wq, bq, wk, wv, bv, wo, bo, gain, shift, of
 
             def out_unit(jb, hf):
                 if hf == 0:
-                    z_of[jb] = last.tile([P, D], F32, name="z", tag="z")
-                z = z_of[jb]
+                    z_of[jb] = (
+                        last.tile([P, D], F32, name="z", tag="z"),
+                        small.tile([P, 2, 6], F32, name="stats", tag="stats"),
+                    )
+                z = z_of[jb][0]
                 feats = slice(hf * VW, (hf + 1) * VW)
                 o_ps = psum_large.tile([P, VW], F32, tag="large")
                 for c in range(CB):
@@ -262,33 +266,39 @@ def tile_bert_b_kernel(tc, tok, pos, wq, bq, wk, wv, bv, wo, bo, gain, shift, of
                     )
                 nc.vector.tensor_tensor(z[:, feats], o_ps[:], xT[:, jb, feats], ALU.add)
 
+            def statistics(jb, hf):
+                z, stats = z_of[jb]
+                nc.vector.bn_stats(stats[:, hf, :], z[:, hf * VW:(hf + 1) * VW])
+
             def moments(jb):
-                z = z_of[jb]
-                stats = small.tile([P, 2, 6], F32, tag="stats")
-                for hf in range(2):
-                    nc.vector.bn_stats(stats[:, hf, :], z[:, hf * VW:(hf + 1) * VW])
+                stats = z_of[jb][1]
                 mean_var = small.tile([P, 2], F32, tag="mean_var")
                 nc.vector.bn_aggr(mean_var[:], stats[:].rearrange("p a b -> p (a b)"))
                 var_eps = small.tile([P, 1], F32, tag="var_eps")
                 nc.gpsimd.tensor_scalar_add(var_eps[:], mean_var[:, 1:2], EPS)
                 rstd = small.tile([P, 1], F32, tag="rstd")
                 nc.gpsimd.tensor_tensor(rstd[:], var_eps[:], minus_half[:], ALU.pow)
-                minus_mu_rstd = small.tile([P, 1], F32, tag="minus_mu_rstd")
-                nc.gpsimd.tensor_scalar(
-                    minus_mu_rstd[:], mean_var[:, 0:1], rstd[:], -1.0, op0=ALU.mult, op1=ALU.mult
-                )
-                moments_of[jb] = (rstd, minus_mu_rstd)
+                minus_mu_rstd = None
+                if jb < TB - 1:
+                    minus_mu_rstd = small.tile([P, 1], F32, name="minus_mu_rstd", tag="minus_mu_rstd")
+                    nc.gpsimd.tensor_scalar(
+                        minus_mu_rstd[:], mean_var[:, 0:1], rstd[:], -1.0, op0=ALU.mult, op1=ALU.mult
+                    )
+                moments_of[jb] = (mean_var[:, 0:1], rstd, minus_mu_rstd)
 
             def normalise(jb):
-                z = z_of[jb]
-                rstd, minus_mu_rstd = moments_of[jb]
+                z = z_of[jb][0]
+                mu, rstd, minus_mu_rstd = moments_of[jb]
                 normed = last.tile([P, D], F32, tag="normed")
-                nc.scalar.activation(normed[:], z[:], ACT.Identity, bias=minus_mu_rstd[:], scale=rstd[:])
+                if jb == TB - 1:
+                    nc.vector.tensor_scalar(normed[:], z[:], mu, rstd[:], op0=ALU.subtract, op1=ALU.mult)
+                else:
+                    nc.scalar.activation(normed[:], z[:], ACT.Identity, bias=minus_mu_rstd[:], scale=rstd[:])
                 normed_of[jb] = normed
 
             def store_block(jb):
                 normed = normed_of[jb]
-                res = last.tile([P, CB, P], F32, tag="res")
+                res = leaving.tile([P, CB, P], F32, tag="res")
                 for g in range(2):
                     back = psum_large.tile([P, 3, P], F32, tag="large")
                     for i in range(3):
@@ -313,6 +323,7 @@ def tile_bert_b_kernel(tc, tok, pos, wq, bq, wk, wv, bv, wo, bo, gain, shift, of
                 if 0 <= jb - 2 < TB:
                     normalise(jb - 2)
                 if 0 <= jb - 1 < TB:
+                    statistics(jb - 1, 1)
                     moments(jb - 1)
                 if odd and 0 <= pair + 3 < PAIRS:
                     project_k(pair + 3)
@@ -327,6 +338,7 @@ def tile_bert_b_kernel(tc, tok, pos, wq, bq, wk, wv, bv, wo, bo, gain, shift, of
                 if not odd and 0 <= s + 4 < V_UNITS:
                     value_unit(s + 5)
                 if 0 <= jb < TB:
+                    statistics(jb, 0)
                     out_unit(jb, 1)
                 if 0 <= s < UNITS:
                     context(s)

@@ -48,9 +48,7 @@ def tile_bert_b_kernel(tc, tok, pos, wq, bq, wk, wv, bv, wo, bo, gain, shift, of
         for i, vec in enumerate((bq, gain, shift)):
             nc.scalar.dma_start(rows[i * CB:(i + 1) * CB, :], vec.rearrange("(b p) o -> b (p o)", p=P))
         bv_bc = held.tile([P, D], F32, name="bv_bc")
-        nc.gpsimd.dma_start(bv_bc[:], bv.rearrange("d o -> (d o)").partition_broadcast(P))
         bo_bc = held.tile([P, D], F32, name="bo_bc")
-        nc.gpsimd.dma_start(bo_bc[:], bo.rearrange("d o -> (d o)").partition_broadcast(P))
 
         ident_f = held.tile([P, P], F32, name="ident_f")
         make_identity(nc, ident_f[:])
@@ -93,6 +91,8 @@ def tile_bert_b_kernel(tc, tok, pos, wq, bq, wk, wv, bv, wo, bo, gain, shift, of
                 if c > 0:
                     nc.sync.dma_start(w_t["wq"][c - 1][:], wq[(c - 1) * P:c * P, :])
             nc.sync.dma_start(w_t["wq"][CB - 1][:], wq[(CB - 1) * P:, :])
+            nc.sync.dma_start(bo_bc[:], bo.rearrange("d o -> (d o)").partition_broadcast(P))
+            nc.sync.dma_start(bv_bc[:], bv.rearrange("d o -> (d o)").partition_broadcast(P))
             for name, w in (("wk", wk), ("wv", wv), ("wo", wo)):
                 for c in range(CB):
                     nc.sync.dma_start(w_t[name][c][:], w[c * P:(c + 1) * P, :])

@@ -66,10 +66,9 @@ def tile_bert_b_kernel(tc, tok, pos, wq, bq, wk, wv, bv, wo, bo, gain, shift, of
         gain_col = [cols[:, 1 * CB + b:1 * CB + b + 1] for b in range(CB)]
         shift_col = [cols[:, 2 * CB + b:2 * CB + b + 1] for b in range(CB)]
 
-        w_t = {
-            name: [held.tile([P, D], BF16, name=f"{name}_{c}") for c in range(CB)]
-            for name in ("wq", "wk", "wv", "wo")
-        }
+        whole = {name: held.tile([P, CB, D], BF16, name=f"{name}_whole") for name in ("wk", "wv", "wo")}
+        w_t = {name: [whole[name][:, c, :] for c in range(CB)] for name in ("wk", "wv", "wo")}
+        w_t["wq"] = [held.tile([P, D], BF16, name=f"wq_{c}")[:] for c in range(CB)]
         x32 = [held.tile([P, N], F32, name=f"x32_{c}") for c in range(CB)]
         xb = [held.tile([P, N], BF16, name=f"xb_{c}") for c in range(CB)]
         xT = held.tile([P, TB, D], F32, name="xT")
@@ -89,13 +88,13 @@ def tile_bert_b_kernel(tc, tok, pos, wq, bq, wk, wv, bv, wo, bo, gain, shift, of
                 nc.sync.dma_start(pos_t[c][:], pos[block, :])
                 nc.sync.dma_start(tok_t[c][:], tok[block, :])
                 if c > 0:
-                    nc.sync.dma_start(w_t["wq"][c - 1][:], wq[(c - 1) * P:c * P, :])
-            nc.sync.dma_start(w_t["wq"][CB - 1][:], wq[(CB - 1) * P:, :])
+                    nc.sync.dma_start(w_t["wq"][c - 1], wq[(c - 1) * P:c * P, :])
+            nc.sync.dma_start(w_t["wq"][CB - 1], wq[(CB - 1) * P:, :])
             nc.sync.dma_start(bo_bc[:], bo.rearrange("d o -> (d o)").partition_broadcast(P))
+            nc.sync.dma_start(whole["wk"][:], wk.rearrange("(c p) m -> p c m", p=P))
+            nc.sync.dma_start(whole["wv"][:], wv.rearrange("(c p) m -> p c m", p=P))
             nc.sync.dma_start(bv_bc[:], bv.rearrange("d o -> (d o)").partition_broadcast(P))
-            for name, w in (("wk", wk), ("wv", wv), ("wo", wo)):
-                for c in range(CB):
-                    nc.sync.dma_start(w_t[name][c][:], w[c * P:(c + 1) * P, :])
+            nc.sync.dma_start(whole["wo"][:], wo.rearrange("(c p) m -> p c m", p=P))
 
             q_first = [psum_first.tile([P, HALF], F32, name=f"q_first_{pair}") for pair in range(EARLY)]
             for c in range(CB):

@@ -328,14 +328,14 @@ def tile_bert_b_kernel(tc, tok, pos, wq, bq, wk, wv, bv, wo, bo, gain, shift, of
                     project_k(pair + 3)
                 if not odd and EARLY <= pair + 2 < PAIRS:
                     project_q(pair + 2)
-                if not odd and 0 <= s + 4 < V_UNITS:
-                    value_unit(s + 4)
+                if not odd and 0 <= s + 2 < V_UNITS:
+                    value_unit(s + 2)
                 if 0 <= jb < TB:
                     out_unit(jb, 0)
                 if 0 <= s + 2 < UNITS:
                     softmax_bottom(s + 2)
-                if not odd and 0 <= s + 4 < V_UNITS:
-                    value_unit(s + 5)
+                if not odd and 0 <= s + 2 < V_UNITS:
+                    value_unit(s + 3)
                 if 0 <= jb < TB:
                     statistics(jb, 0)
                     out_unit(jb, 1)

import math

import concourse.mybir as mybir
from concourse.masks import make_identity

F32 = mybir.dt.float32
BF16 = mybir.dt.bfloat16
U16 = mybir.dt.uint16
ALU = mybir.AluOpType
ACT = mybir.ActivationFunctionType
AX = mybir.AxisListType

P = 128
D = 768
V = 2048
N = 1024
SQ = 256
NB = N // SQ
NH = D // P
CB = D // P
HALF = 512
LW = SQ // 16
TB = N // P
VW = D // 2
UNITS = NB * NH
PAIRS = UNITS // 2
V_UNITS = TB * 2
EARLY = 8
FIRST_OUT = 2 * (PAIRS - 3) + 1
EPS = 1e-5
SCALE = 1.0 / math.sqrt(P)

FLOPS = 4 * 2 * D * D * N + 2 * 2 * NH * NB * SQ * SQ * P


def tile_bert_b_kernel(tc, tok, pos, wq, bq, wk, wv, bv, wo, bo, gain, shift, offs, out):
    nc = tc.nc
    with (
        tc.tile_pool(name="held", bufs=1) as held,
        tc.tile_pool(name="work", bufs=3) as work,
        tc.tile_pool(name="small", bufs=4) as small,
    ):
        offsets = held.tile([P, N // 16], U16, name="offsets")
        nc.sync.dma_start(offsets[:], offs)

        rows = held.tile([P, P], F32, name="rows")
        nc.gpsimd.memset(rows[:], 0.0)
        for i, vec in enumerate((bq, gain, shift)):
            nc.scalar.dma_start(rows[i * CB:(i + 1) * CB, :], vec.rearrange("(b p) o -> b (p o)", p=P))
        bv_bc = held.tile([P, D], F32, name="bv_bc")
        bo_bc = held.tile([P, D], F32, name="bo_bc")

        ident_f = held.tile([P, P], F32, name="ident_f")
        make_identity(nc, ident_f[:])
        ident_b = held.tile([P, P], BF16, name="ident_b")
        make_identity(nc, ident_b[:])
        minus_half = held.tile([P, 1], F32, name="minus_half")
        nc.gpsimd.memset(minus_half[:], -0.5)

        cols = held.tile([P, P], F32, name="cols")
        with tc.psum_pool(name="psum_cols", bufs=1) as psum_cols:
            cols_ps = psum_cols.tile([P, P], F32, name="cols_ps")
            nc.tensor.transpose(cols_ps[:], rows[:], ident_f[:])
            nc.scalar.copy(cols[:], cols_ps[:])
        bq_col = [cols[:, 0 * CB + b:0 * CB + b + 1] for b in range(CB)]
        gain_col = [cols[:, 1 * CB + b:1 * CB + b + 1] for b in range(CB)]
        shift_col = [cols[:, 2 * CB + b:2 * CB + b + 1] for b in range(CB)]

        whole = {name: held.tile([P, CB, D], BF16, name=f"{name}_whole") for name in ("wk", "wv", "wo")}
        w_t = {name: [whole[name][:, c, :] for c in range(CB)] for name in ("wk", "wv", "wo")}
        w_t["wq"] = [held.tile([P, D], BF16, name=f"wq_{c}")[:] for c in range(CB)]
        x32 = [held.tile([P, N], F32, name=f"x32_{c}") for c in range(CB)]
        xb = [held.tile([P, N], BF16, name=f"xb_{c}") for c in range(CB)]
        xT = held.tile([P, TB, D], F32, name="xT")
        q_t = [held.tile([P, N], BF16, name=f"q_{h}") for h in range(NH)]
        k_t = [held.tile([P, N], BF16, name=f"k_{h}") for h in range(NH)]
        vT = [held.tile([P, D], BF16, name=f"vT_{jb}") for jb in range(TB)]
        ctx = [held.tile([P, N], BF16, name=f"ctx_{h}") for h in range(NH)]

        with (
            tc.tile_pool(name="table", bufs=1) as table,
            tc.psum_pool(name="psum_first", bufs=1) as psum_first,
        ):
            tok_t = [table.tile([P, V], F32, name=f"tok_{c}") for c in range(CB)]
            pos_t = [table.tile([P, SQ], F32, name=f"pos_{c}") for c in range(CB)]
            for c in range(CB):
                block = slice(c * P, (c + 1) * P)
                nc.sync.dma_start(pos_t[c][:], pos[block, :])
                nc.sync.dma_start(tok_t[c][:], tok[block, :])
                if c > 0:
                    nc.sync.dma_start(w_t["wq"][c - 1], wq[(c - 1) * P:c * P, :])
            nc.sync.dma_start(w_t["wq"][CB - 1], wq[(CB - 1) * P:, :])
            nc.sync.dma_start(bo_bc[:], bo.rearrange("d o -> (d o)").partition_broadcast(P))
            nc.sync.dma_start(whole["wk"][:], wk.rearrange("(c p) m -> p c m", p=P))
            nc.sync.dma_start(whole["wv"][:], wv.rearrange("(c p) m -> p c m", p=P))
            nc.sync.dma_start(bv_bc[:], bv.rearrange("d o -> (d o)").partition_broadcast(P))
            nc.sync.dma_start(whole["wo"][:], wo.rearrange("(c p) m -> p c m", p=P))

            q_first = [psum_first.tile([P, HALF], F32, name=f"q_first_{pair}") for pair in range(EARLY)]
            for c in range(CB):
                for r in range(NB):
                    nc.vector.tensor_tensor(
                        x32[c][:, r * SQ:(r + 1) * SQ],
                        tok_t[c][:].indirect(offsets[:, r * LW:(r + 1) * LW]),
                        pos_t[c][:],
                        ALU.add,
                    )
                    if r % 2 == 1:
                        span = slice((r - 1) * SQ, (r + 1) * SQ)
                        nc.scalar.copy(xb[c][:, span], x32[c][:, span])
                for pair in range(EARLY):
                    half, h = divmod(pair, NH)
                    nc.tensor.matmul(
                        q_first[pair][:],
                        lhsT=w_t["wq"][c][:, h * P:(h + 1) * P], rhs=xb[c][:, half * HALF:(half + 1) * HALF],
                        start=(c == 0), stop=(c == CB - 1),
                    )

            for pair in range(EARLY):
                half, h = divmod(pair, NH)
                q_out = q_t[h][:, half * HALF:(half + 1) * HALF]
                if pair % 2 == 0:
                    nc.scalar.activation(q_out, q_first[pair][:], ACT.Identity, bias=bq_col[h])
                else:
                    nc.vector.tensor_scalar_add(q_out, q_first[pair][:], bq_col[h])

        with (
            tc.tile_pool(name="last", bufs=3) as last,
            tc.tile_pool(name="leaving", bufs=4) as leaving,
            tc.psum_pool(name="psum_large", bufs=4) as psum_large,
            tc.psum_pool(name="psum_sc", bufs=2) as psum_sc,
            tc.psum_pool(name="psum_flip", bufs=1) as psum_flip,
            tc.psum_pool(name="psum_ctx", bufs=1) as psum_ctx,
        ):
            def flip_x(c):
                bo_block = bo_bc[:, c * P:(c + 1) * P].unsqueeze(1).to_broadcast([P, 4, P])
                for g in range(TB // 4):
                    xT_ps = psum_large.tile([P, 4, P], F32, tag="large")
                    for i in range(4):
                        jb = 4 * g + i
                        nc.tensor.transpose(xT_ps[:, i, :], x32[c][:, jb * P:(jb + 1) * P], ident_f[:])
                    nc.vector.tensor_tensor(xT[:, 4 * g:4 * g + 4, c * P:(c + 1) * P], xT_ps[:], bo_block, ALU.add)

            def where(u):
                pair, second = divmod(u, 2)
                half, h = divmod(pair, NH)
                return h, 2 * half + second

            def project(name, pair):
                half, h = divmod(pair, NH)
                acc = psum_large.tile([P, HALF], F32, name="acc", tag="large")
                for c in range(CB):
                    nc.tensor.matmul(
                        acc[:], lhsT=w_t[name][c][:, h * P:(h + 1) * P], rhs=xb[c][:, half * HALF:(half + 1) * HALF],
                        start=(c == 0), stop=(c == CB - 1),
                    )
                return acc

            def project_q(pair):
                half, h = divmod(pair, NH)
                nc.scalar.activation(
                    q_t[h][:, half * HALF:(half + 1) * HALF], project("wq", pair)[:], ACT.Identity, bias=bq_col[h]
                )

            def project_k(pair):
                half, h = divmod(pair, NH)
                nc.scalar.copy(k_t[h][:, half * HALF:(half + 1) * HALF], project("wk", pair)[:])

            sc_of = {}
            e_of = {}
            att_of = {}
            attT_of = {}

            def scores(u):
                h, r = where(u)
                sc = psum_sc.tile([P, 2, SQ], F32, tag="sc")
                for tb in range(2):
                    nc.tensor.matmul(
                        sc[:, tb, :],
                        lhsT=q_t[h][:, r * SQ + tb * P:r * SQ + (tb + 1) * P],
                        rhs=k_t[h][:, r * SQ:(r + 1) * SQ],
                        start=True, stop=True,
                    )
                sc_of[u] = sc

            def softmax_top(u):
                sc = sc_of[u]
                top = small.tile([P, 2], F32, tag="top")
                nc.vector.tensor_reduce(top[:], sc[:], axis=AX.X, op=ALU.max)
                shift_exp = small.tile([P, 2], F32, tag="shift_exp")
                nc.vector.tensor_scalar_mul(shift_exp[:], top[:], -SCALE)
                e = work.tile([P, 2, SQ], F32, tag="e")
                e_sum = small.tile([P, 2], F32, tag="e_sum")
                for tb in range(2):
                    nc.scalar.activation(
                        e[:, tb, :], sc[:, tb, :], ACT.Exp,
                        bias=shift_exp[:, tb:tb + 1], scale=SCALE, accum_out=e_sum[:, tb:tb + 1],
                    )
                e_of[u] = (e, e_sum)

            def softmax_bottom(u):
                e, e_sum = e_of[u]
                e_inv = small.tile([P, 2], F32, tag="e_inv")
                nc.vector.reciprocal(e_inv[:], e_sum[:])
                att = work.tile([P, 2, SQ], BF16, tag="att")
                for tb in range(2):
                    nc.vector.tensor_scalar_mul(att[:, tb, :], e[:, tb, :], e_inv[:, tb:tb + 1])
                att_of[u] = att

            def flip(u):
                att = att_of[u]
                attT_ps = psum_flip.tile([P, 2, SQ], BF16, tag="attT_ps")
                for ub in range(2):
                    for tb in range(2):
                        nc.tensor.transpose(
                            attT_ps[:, ub, tb * P:(tb + 1) * P], att[:, tb, ub * P:(ub + 1) * P], ident_b[:]
                        )
                attT = work.tile([P, 2, SQ], BF16, tag="attT")
                nc.scalar.copy(attT[:], attT_ps[:])
                attT_of[u] = attT

            def context(u):
                h, r = where(u)
                attT = attT_of[u]
                ctx_ps = psum_ctx.tile([P, SQ], F32, tag="ctx_ps")
                for ub in range(2):
                    nc.tensor.matmul(
                        ctx_ps[:],
                        lhsT=vT[r * 2 + ub][:, h * P:(h + 1) * P],
                        rhs=attT[:, ub, :],
                        start=(ub == 0), stop=(ub == 1),
                    )
                nc.scalar.copy(ctx[h][:, r * SQ:(r + 1) * SQ], ctx_ps[:])

            def value_unit(n):
                group, k = divmod(n, TB // 2)
                half, hf = divmod(group, 2)
                jb = half * (TB // 2) + k
                feats = slice(hf * VW, (hf + 1) * VW)
                v_ps = psum_large.tile([P, VW], F32, tag="large")
                for c in range(CB):
                    nc.tensor.matmul(
                        v_ps[:], lhsT=xb[c][:, jb * P:(jb + 1) * P], rhs=w_t["wv"][c][:, feats],
                        start=(c == 0), stop=(c == CB - 1),
                    )
                nc.vector.tensor_tensor(vT[jb][:, feats], v_ps[:], bv_bc[:, feats], ALU.add)

            z_of = {}
            moments_of = {}
            normed_of = {}

            def out_unit(jb, hf):
                if hf == 0:
                    z_of[jb] = (
                        last.tile([P, D], F32, name="z", tag="z"),
                        small.tile([P, 2, 6], F32, name="stats", tag="stats"),
                    )
                z = z_of[jb][0]
                feats = slice(hf * VW, (hf + 1) * VW)
                o_ps = psum_large.tile([P, VW], F32, tag="large")
                for c in range(CB):
                    nc.tensor.matmul(
                        o_ps[:], lhsT=ctx[c][:, jb * P:(jb + 1) * P], rhs=w_t["wo"][c][:, feats],
                        start=(c == 0), stop=(c == CB - 1),
                    )
                nc.vector.tensor_tensor(z[:, feats], o_ps[:], xT[:, jb, feats], ALU.add)

            def statistics(jb, hf):
                z, stats = z_of[jb]
                nc.vector.bn_stats(stats[:, hf, :], z[:, hf * VW:(hf + 1) * VW])

            def moments(jb):
                stats = z_of[jb][1]
                mean_var = small.tile([P, 2], F32, tag="mean_var")
                nc.vector.bn_aggr(mean_var[:], stats[:].rearrange("p a b -> p (a b)"))
                var_eps = small.tile([P, 1], F32, tag="var_eps")
                nc.gpsimd.tensor_scalar_add(var_eps[:], mean_var[:, 1:2], EPS)
                rstd = small.tile([P, 1], F32, tag="rstd")
                nc.gpsimd.tensor_tensor(rstd[:], var_eps[:], minus_half[:], ALU.pow)
                minus_mu_rstd = None
                if jb < TB - 1:
                    minus_mu_rstd = small.tile([P, 1], F32, name="minus_mu_rstd", tag="minus_mu_rstd")
                    nc.gpsimd.tensor_scalar(
                        minus_mu_rstd[:], mean_var[:, 0:1], rstd[:], -1.0, op0=ALU.mult, op1=ALU.mult
                    )
                moments_of[jb] = (mean_var[:, 0:1], rstd, minus_mu_rstd)

            def normalise(jb):
                z = z_of[jb][0]
                mu, rstd, minus_mu_rstd = moments_of[jb]
                normed = last.tile([P, D], F32, tag="normed")
                if jb == TB - 1:
                    nc.vector.tensor_scalar(normed[:], z[:], mu, rstd[:], op0=ALU.subtract, op1=ALU.mult)
                else:
                    nc.scalar.activation(normed[:], z[:], ACT.Identity, bias=minus_mu_rstd[:], scale=rstd[:])
                normed_of[jb] = normed

            def store_block(jb):
                normed = normed_of[jb]
                res = leaving.tile([P, CB, P], F32, tag="res")
                for g in range(2):
                    back = psum_large.tile([P, 3, P], F32, tag="large")
                    for i in range(3):
                        m = 3 * g + i
                        nc.tensor.transpose(back[:, i, :], normed[:, m * P:(m + 1) * P], ident_f[:])
                    for i in range(3):
                        m = 3 * g + i
                        nc.scalar.activation(
                            res[:, m, :], back[:, i, :], ACT.Identity, bias=shift_col[m], scale=gain_col[m]
                        )
                nc.sync.dma_start(out.rearrange("(m p) j -> p m j", p=P)[:, :, jb * P:(jb + 1) * P], res[:])

            for s in range(-CB, FIRST_OUT + TB + 3):
                pair, odd = divmod(s, 2)
                jb = s - FIRST_OUT
                if s < 0:
                    flip_x(s + CB)
                if 0 <= s < UNITS:
                    flip(s)
                if 0 <= s + 2 < UNITS:
                    softmax_top(s + 2)
                if 0 <= jb - 2 < TB:
                    normalise(jb - 2)
                if 0 <= jb - 1 < TB:
                    statistics(jb - 1, 1)
                    moments(jb - 1)
                if odd and 0 <= pair + 3 < PAIRS:
                    project_k(pair + 3)
                if not odd and EARLY <= pair + 2 < PAIRS:
                    project_q(pair + 2)
                if not odd and 0 <= s + 2 < V_UNITS:
                    value_unit(s + 2)
                if 0 <= jb < TB:
                    out_unit(jb, 0)
                if 0 <= s + 2 < UNITS:
                    softmax_bottom(s + 2)
                if not odd and 0 <= s + 2 < V_UNITS:
                    value_unit(s + 3)
                if 0 <= jb < TB:
                    statistics(jb, 0)
                    out_unit(jb, 1)
                if 0 <= s < UNITS:
                    context(s)
                if 0 <= s + 3 < UNITS:
                    scores(s + 3)
                if 0 <= jb - 3 < TB:
                    store_block(jb - 3)
